import numpy as np
import ml_dtypes

BF16 = ml_dtypes.bfloat16


def bf(x):
    return np.asarray(x, np.float32).astype(BF16)


def f32(x):
    return np.asarray(x, np.float32)


def f64(x):
    return np.asarray(x).astype(np.float64)


def striped(idx):
    return np.tile(idx.reshape(-1, 16).T, (8, 1))


C, D, R, HF, S, N = 256, 128, 64, 32, 512, 64
BASE = 10000.0


def rope_tables():
    inv_freq = 1.0 / (BASE ** (np.arange(0, R, R // HF, dtype=np.float32) / R))
    t = np.arange(S, dtype=np.float32)
    freqs = np.einsum('i,j->ij', t, inv_freq)
    emb = np.concatenate([freqs, freqs], axis=-1)
    return np.cos(emb), np.sin(emb)


def rotate_half(v):
    b = v.reshape(D // R, R // HF, HF, -1)
    return np.concatenate([-b[:, 1], b[:, 0]], axis=1).reshape(D, -1)


def setup_inputs():
    cos_t, sin_t = rope_tables()
    tab = np.concatenate([cos_t.T] * (D // R) + [sin_t.T] * (D // R), axis=0)
    return {"x": f32(np.random.standard_normal((D, N))), "tab": f32(tab), "offs": striped(np.random.permutation(np.tile(np.arange(S), 2))[:N])}


def reference(x, tab, offs):
    idx = offs[:16].T.reshape(-1)
    t = f64(tab)[:, idx]
    v = f64(x)
    return v * t[:D] + rotate_half(v) * t[D:]

@@ -1,0 +1,44 @@
+import concourse.mybir as mybir
+
+F32 = mybir.dt.float32
+U16 = mybir.dt.uint16
+MULT = mybir.AluOpType.mult
+ADD = mybir.AluOpType.add
+
+P = 128
+N = 64
+POSITIONS = 512
+BLOCK = 64
+HALF = 32
+
+
+def tile_selfattention_kernel(tc, x, tab, offs, out):
+    nc = tc.nc
+    with tc.tile_pool(name="held", bufs=1) as held:
+        offsets = held.tile([P, N // 16], U16, name="offsets")
+        x_rows = held.tile([P, N], F32, name="x_rows")
+        rotated = held.tile([P, N], F32, name="rotated")
+        cosines = held.tile([P, POSITIONS], F32, name="cosines")
+        sines = held.tile([P, POSITIONS], F32, name="sines")
+        by_cos = held.tile([P, N], F32, name="by_cos")
+        by_sin = held.tile([P, N], F32, name="by_sin")
+        result = held.tile([P, N], F32, name="result")
+
+        nc.sync.dma_start(offsets[:], offs)
+        nc.sync.dma_start(x_rows[:], x)
+        nc.sync.dma_start(cosines[:], tab[0:P, :])
+
+        for first in range(0, P, BLOCK):
+            second = first + HALF
+            nc.scalar.dma_start(rotated[first : first + HALF, :], x[second : second + HALF, :])
+            nc.scalar.dma_start(rotated[second : second + HALF, :], x[first : first + HALF, :])
+        nc.scalar.dma_start(sines[:], tab[P : 2 * P, :])
+
+        for first in range(0, P, BLOCK):
+            lower = rotated[first : first + HALF, :]
+            nc.vector.tensor_scalar_mul(lower, lower, -1.0)
+
+        nc.vector.tensor_tensor(by_cos[:], cosines[:].indirect(offsets[:]), x_rows[:], MULT)
+        nc.vector.tensor_tensor(by_sin[:], sines[:].indirect(offsets[:]), rotated[:], MULT)
+        nc.vector.tensor_tensor(result[:], by_cos[:], by_sin[:], ADD)
+        nc.sync.dma_start(out, result[:])

@@ -17,7 +17,8 @@ def tile_selfattention_kernel(tc, x, tab, offs, out):
     with tc.tile_pool(name="held", bufs=1) as held:
         offsets = held.tile([P, N // 16], U16, name="offsets")
         x_rows = held.tile([P, N], F32, name="x_rows")
-        rotated = held.tile([P, N], F32, name="rotated")
+        swapped = held.tile([P, N], F32, name="swapped")
+        sign = held.tile([P, 1], F32, name="sign")
         cosines = held.tile([P, POSITIONS], F32, name="cosines")
         sines = held.tile([P, POSITIONS], F32, name="sines")
         by_cos = held.tile([P, N], F32, name="by_cos")
@@ -30,15 +31,15 @@ def tile_selfattention_kernel(tc, x, tab, offs, out):
 
         for first in range(0, P, BLOCK):
             second = first + HALF
-            nc.scalar.dma_start(rotated[first : first + HALF, :], x[second : second + HALF, :])
-            nc.scalar.dma_start(rotated[second : second + HALF, :], x[first : first + HALF, :])
+            nc.scalar.dma_start(swapped[first : first + HALF, :], x[second : second + HALF, :])
+            nc.scalar.dma_start(swapped[second : second + HALF, :], x[first : first + HALF, :])
         nc.scalar.dma_start(sines[:], tab[P : 2 * P, :])
 
+        nc.vector.memset(sign[:], 1.0)
         for first in range(0, P, BLOCK):
-            lower = rotated[first : first + HALF, :]
-            nc.vector.tensor_scalar_mul(lower, lower, -1.0)
+            nc.vector.memset(sign[first : first + HALF, :], -1.0)
 
         nc.vector.tensor_tensor(by_cos[:], cosines[:].indirect(offsets[:]), x_rows[:], MULT)
-        nc.vector.tensor_tensor(by_sin[:], sines[:].indirect(offsets[:]), rotated[:], MULT)
-        nc.vector.tensor_tensor(result[:], by_cos[:], by_sin[:], ADD)
+        nc.vector.tensor_tensor(by_sin[:], sines[:].indirect(offsets[:]), swapped[:], MULT)
+        nc.vector.scalar_tensor_tensor(result[:], by_sin[:], sign[:, 0:1], by_cos[:], MULT, ADD)
         nc.sync.dma_start(out, result[:])

@@ -10,20 +10,21 @@ N = 64
 POSITIONS = 512
 BLOCK = 64
 HALF = 32
+AXI = 256
 
 
 def tile_selfattention_kernel(tc, x, tab, offs, out):
     nc = tc.nc
     with tc.tile_pool(name="held", bufs=1) as held:
         offsets = held.tile([P, N // 16], U16, name="offsets")
-        x_rows = held.tile([P, N], F32, name="x_rows")
-        swapped = held.tile([P, N], F32, name="swapped")
+        x_rows = held.tile([P, N], F32, name="x_rows", align_bytes=AXI)
+        swapped = held.tile([P, N], F32, name="swapped", align_bytes=AXI)
         sign = held.tile([P, 1], F32, name="sign")
-        cosines = held.tile([P, POSITIONS], F32, name="cosines")
-        sines = held.tile([P, POSITIONS], F32, name="sines")
+        cosines = held.tile([P, POSITIONS], F32, name="cosines", align_bytes=AXI)
+        sines = held.tile([P, POSITIONS], F32, name="sines", align_bytes=AXI)
         by_cos = held.tile([P, N], F32, name="by_cos")
         by_sin = held.tile([P, N], F32, name="by_sin")
-        result = held.tile([P, N], F32, name="result")
+        result = held.tile([P, N], F32, name="result", align_bytes=AXI)
 
         nc.sync.dma_start(offsets[:], offs)
         nc.sync.dma_start(x_rows[:], x)

@@ -4,6 +4,7 @@ F32 = mybir.dt.float32
 U16 = mybir.dt.uint16
 MULT = mybir.AluOpType.mult
 ADD = mybir.AluOpType.add
+SUBTRACT = mybir.AluOpType.subtract
 
 P = 128
 N = 64
@@ -17,30 +18,32 @@ def tile_selfattention_kernel(tc, x, tab, offs, out):
     nc = tc.nc
     with tc.tile_pool(name="held", bufs=1) as held:
         offsets = held.tile([P, N // 16], U16, name="offsets")
-        x_rows = held.tile([P, N], F32, name="x_rows", align_bytes=AXI)
-        swapped = held.tile([P, N], F32, name="swapped", align_bytes=AXI)
-        sign = held.tile([P, 1], F32, name="sign")
+        places = held.tile([P, 3 * N], F32, name="places", align_bytes=AXI)
         cosines = held.tile([P, POSITIONS], F32, name="cosines", align_bytes=AXI)
         sines = held.tile([P, POSITIONS], F32, name="sines", align_bytes=AXI)
+        result = held.tile([P, N], F32, name="result", align_bytes=AXI)
+        rotated = held.tile([P, N], F32, name="rotated")
         by_cos = held.tile([P, N], F32, name="by_cos")
         by_sin = held.tile([P, N], F32, name="by_sin")
-        result = held.tile([P, N], F32, name="result", align_bytes=AXI)
 
         nc.sync.dma_start(offsets[:], offs)
-        nc.sync.dma_start(x_rows[:], x)
         nc.sync.dma_start(cosines[:], tab[0:P, :])
 
         for first in range(0, P, BLOCK):
-            second = first + HALF
-            nc.scalar.dma_start(swapped[first : first + HALF, :], x[second : second + HALF, :])
-            nc.scalar.dma_start(swapped[second : second + HALF, :], x[first : first + HALF, :])
+            pair = x[first : first + BLOCK, :].rearrange("(t r) n -> r t n", t=2)
+            for half in range(2):
+                rows = slice(first + half * HALF, first + (half + 1) * HALF)
+                columns = slice((1 - half) * N, (3 - half) * N)
+                nc.scalar.dma_start(places[rows, columns].rearrange("p (t n) -> p t n", t=2), pair)
         nc.scalar.dma_start(sines[:], tab[P : 2 * P, :])
+        x_rows = places[:, N : 2 * N]
 
-        nc.vector.memset(sign[:], 1.0)
         for first in range(0, P, BLOCK):
-            nc.vector.memset(sign[first : first + HALF, :], -1.0)
+            nc.vector.memset(places[first : first + HALF, 0:N], 0.0)
+            nc.vector.memset(places[first + HALF : first + BLOCK, 2 * N : 3 * N], 0.0)
+        nc.vector.tensor_tensor(rotated[:], places[:, 0:N], places[:, 2 * N : 3 * N], SUBTRACT)
 
-        nc.vector.tensor_tensor(by_cos[:], cosines[:].indirect(offsets[:]), x_rows[:], MULT)
-        nc.vector.tensor_tensor(by_sin[:], sines[:].indirect(offsets[:]), swapped[:], MULT)
-        nc.vector.scalar_tensor_tensor(result[:], by_sin[:], sign[:, 0:1], by_cos[:], MULT, ADD)
+        nc.vector.tensor_tensor(by_cos[:], cosines[:].indirect(offsets[:]), x_rows, MULT)
+        nc.vector.tensor_tensor(by_sin[:], sines[:].indirect(offsets[:]), rotated[:], MULT)
+        nc.vector.tensor_tensor(result[:], by_cos[:], by_sin[:], ADD)
         nc.sync.dma_start(out, result[:])

@@ -12,6 +12,7 @@ POSITIONS = 512
 BLOCK = 64
 HALF = 32
 AXI = 256
+TABLE_ROW = 4 * POSITIONS
 
 
 def tile_selfattention_kernel(tc, x, tab, offs, out):
@@ -19,8 +20,8 @@ def tile_selfattention_kernel(tc, x, tab, offs, out):
     with tc.tile_pool(name="held", bufs=1) as held:
         offsets = held.tile([P, N // 16], U16, name="offsets")
         places = held.tile([P, 3 * N], F32, name="places", align_bytes=AXI)
-        cosines = held.tile([P, POSITIONS], F32, name="cosines", align_bytes=AXI)
-        sines = held.tile([P, POSITIONS], F32, name="sines", align_bytes=AXI)
+        cosines = held.tile([P, POSITIONS], F32, name="cosines", align_bytes=TABLE_ROW)
+        sines = held.tile([P, POSITIONS], F32, name="sines", align_bytes=TABLE_ROW)
         result = held.tile([P, N], F32, name="result", align_bytes=AXI)
         rotated = held.tile([P, N], F32, name="rotated")
         by_cos = held.tile([P, N], F32, name="by_cos")

@@ -9,10 +9,14 @@ SUBTRACT = mybir.AluOpType.subtract
 P = 128
 N = 64
 POSITIONS = 512
-BLOCK = 64
-HALF = 32
+BLOCKS = 2
+HALVES = 2 * BLOCKS
 AXI = 256
 TABLE_ROW = 4 * POSITIONS
+
+
+def interleaved(rows):
+    return rows.rearrange("(b u) n -> u b n", b=BLOCKS)
 
 
 def tile_selfattention_kernel(tc, x, tab, offs, out):
@@ -26,25 +30,23 @@ def tile_selfattention_kernel(tc, x, tab, offs, out):
         rotated = held.tile([P, N], F32, name="rotated")
         by_cos = held.tile([P, N], F32, name="by_cos")
         by_sin = held.tile([P, N], F32, name="by_sin")
+        first_halves = slice(0, P // 2)
+        second_halves = slice(P // 2, P)
 
         nc.sync.dma_start(offsets[:], offs)
-        nc.sync.dma_start(cosines[:], tab[0:P, :])
+        nc.sync.dma_start(cosines[:], interleaved(tab[0:P, :]))
 
-        for first in range(0, P, BLOCK):
-            pair = x[first : first + BLOCK, :].rearrange("(t r) n -> r t n", t=2)
-            for half in range(2):
-                rows = slice(first + half * HALF, first + (half + 1) * HALF)
-                columns = slice((1 - half) * N, (3 - half) * N)
-                nc.scalar.dma_start(places[rows, columns].rearrange("p (t n) -> p t n", t=2), pair)
-        nc.scalar.dma_start(sines[:], tab[P : 2 * P, :])
+        pairs = x.rearrange("(q r) n -> r q n", q=HALVES)
+        nc.scalar.dma_start(places[first_halves, N : 3 * N], pairs)
+        nc.scalar.dma_start(places[second_halves, 0 : 2 * N], pairs)
+        nc.scalar.dma_start(sines[:], interleaved(tab[P : 2 * P, :]))
         x_rows = places[:, N : 2 * N]
 
-        for first in range(0, P, BLOCK):
-            nc.vector.memset(places[first : first + HALF, 0:N], 0.0)
-            nc.vector.memset(places[first + HALF : first + BLOCK, 2 * N : 3 * N], 0.0)
+        nc.vector.memset(places[first_halves, 0:N], 0.0)
+        nc.vector.memset(places[second_halves, 2 * N : 3 * N], 0.0)
         nc.vector.tensor_tensor(rotated[:], places[:, 0:N], places[:, 2 * N : 3 * N], SUBTRACT)
 
         nc.vector.tensor_tensor(by_cos[:], cosines[:].indirect(offsets[:]), x_rows, MULT)
         nc.vector.tensor_tensor(by_sin[:], sines[:].indirect(offsets[:]), rotated[:], MULT)
         nc.vector.tensor_tensor(result[:], by_cos[:], by_sin[:], ADD)
-        nc.sync.dma_start(out, result[:])
+        nc.sync.dma_start(interleaved(out), result[:])

@@ -34,11 +34,11 @@ def tile_selfattention_kernel(tc, x, tab, offs, out):
         second_halves = slice(P // 2, P)
 
         nc.sync.dma_start(offsets[:], offs)
-        nc.sync.dma_start(cosines[:], interleaved(tab[0:P, :]))
 
         pairs = x.rearrange("(q r) n -> r q n", q=HALVES)
-        nc.scalar.dma_start(places[first_halves, N : 3 * N], pairs)
+        nc.sync.dma_start(places[first_halves, N : 3 * N], pairs)
         nc.scalar.dma_start(places[second_halves, 0 : 2 * N], pairs)
+        nc.sync.dma_start(cosines[:], interleaved(tab[0:P, :]))
         nc.scalar.dma_start(sines[:], interleaved(tab[P : 2 * P, :]))
         x_rows = places[:, N : 2 * N]
 

import concourse.mybir as mybir

F32 = mybir.dt.float32
U16 = mybir.dt.uint16
MULT = mybir.AluOpType.mult
ADD = mybir.AluOpType.add
SUBTRACT = mybir.AluOpType.subtract

P = 128
N = 64
POSITIONS = 512
BLOCKS = 2
HALVES = 2 * BLOCKS
AXI = 256
TABLE_ROW = 4 * POSITIONS


def interleaved(rows):
    return rows.rearrange("(b u) n -> u b n", b=BLOCKS)


def tile_selfattention_kernel(tc, x, tab, offs, out):
    nc = tc.nc
    with tc.tile_pool(name="held", bufs=1) as held:
        offsets = held.tile([P, N // 16], U16, name="offsets")
        places = held.tile([P, 3 * N], F32, name="places", align_bytes=AXI)
        cosines = held.tile([P, POSITIONS], F32, name="cosines", align_bytes=TABLE_ROW)
        sines = held.tile([P, POSITIONS], F32, name="sines", align_bytes=TABLE_ROW)
        result = held.tile([P, N], F32, name="result", align_bytes=AXI)
        rotated = held.tile([P, N], F32, name="rotated")
        by_cos = held.tile([P, N], F32, name="by_cos")
        by_sin = held.tile([P, N], F32, name="by_sin")
        first_halves = slice(0, P // 2)
        second_halves = slice(P // 2, P)

        nc.sync.dma_start(offsets[:], offs)

        pairs = x.rearrange("(q r) n -> r q n", q=HALVES)
        nc.sync.dma_start(places[first_halves, N : 3 * N], pairs)
        nc.scalar.dma_start(places[second_halves, 0 : 2 * N], pairs)
        nc.sync.dma_start(cosines[:], interleaved(tab[0:P, :]))
        nc.scalar.dma_start(sines[:], interleaved(tab[P : 2 * P, :]))
        x_rows = places[:, N : 2 * N]

        nc.vector.memset(places[first_halves, 0:N], 0.0)
        nc.vector.memset(places[second_halves, 2 * N : 3 * N], 0.0)
        nc.vector.tensor_tensor(rotated[:], places[:, 0:N], places[:, 2 * N : 3 * N], SUBTRACT)

        nc.vector.tensor_tensor(by_cos[:], cosines[:].indirect(offsets[:]), x_rows, MULT)
        nc.vector.tensor_tensor(by_sin[:], sines[:].indirect(offsets[:]), rotated[:], MULT)
        nc.vector.tensor_tensor(result[:], by_cos[:], by_sin[:], ADD)
        nc.sync.dma_start(interleaved(out), result[:])
